import numpy as np
import ml_dtypes


def mxq(x, axis, fmt="e4m3"):
    dtype, down = {"e4m3": (ml_dtypes.float8_e4m3fn, 7), "e5m2": (ml_dtypes.float8_e5m2, 14)}[fmt]
    v = np.moveaxis(np.asarray(x, np.float32).astype(ml_dtypes.bfloat16).astype(np.float64), axis, -1)
    blocks = v.reshape(v.shape[:-1] + (-1, 32))
    amax = np.abs(blocks).max(-1, keepdims=True)
    byte = np.maximum(np.where(amax > 0, np.frexp(amax)[1] - 1 + 127, 0) - down, 1)
    scale = np.exp2(byte - 127.0)
    codes = (blocks / scale).astype(np.float32).astype(dtype).astype(np.float64)
    return np.moveaxis((codes * scale).reshape(v.shape), -1, axis)


WIDE = False


def mx_kscale(k):
    if not WIDE:
        return np.ones(k)
    levels = np.array([20, -20, 10, -10, 0])
    a = np.random.permutation(np.resize(levels, k // 512 * 4)).reshape(k // 512, 4)
    idx = np.arange(k)
    return np.exp2(a[idx // 512, idx % 128 // 32])


BF16 = ml_dtypes.bfloat16


def bf(x):
    return np.asarray(x, np.float32).astype(BF16)


def f64(x):
    return np.asarray(x).astype(np.float64)


N1, N2, N3, R1, R = 512, 32, 512, 512, 512


def setup_inputs():
    s = mx_kscale(N1 * N2)[::N2]
    g = R ** (-1.0 / 6.0)
    X = np.random.standard_normal((N1, N2, N3))
    A = np.random.standard_normal((N1, R)) * g * s[:, None]
    B = np.random.standard_normal((N2, R)) * g
    C = np.random.standard_normal((N3, R)) * g
    go = np.random.standard_normal((N1, N2, N3)) * np.exp2(np.random.randint(-12, 1, (N1, N2, 1))) * 4.0 / s[:, None, None]
    return {"X": bf(X), "A": bf(A), "B": bf(B), "C": bf(C), "grad_out": bf(go)}


def reference(X, A, B, C, grad_out):
    p = (f64(A)[:, None, :] * f64(B)[None, :, :]).reshape(N1 * N2, R)
    g = f64(grad_out).reshape(N1 * N2, N3)
    return mxq(g, 0, "e5m2").T @ mxq(p, 0, "e4m3")

@@ -1,0 +1,128 @@
+import concourse.mybir as mybir
+
+BF16 = mybir.dt.bfloat16
+F32 = mybir.dt.float32
+U32 = mybir.dt.uint32
+U8 = mybir.dt.uint8
+E4M3_X4 = mybir.dt.float8_e4m3fn_x4
+E5M2_X4 = mybir.dt.float8_e5m2_x4
+
+N1, N2, N3, R = 512, 32, 512, 512
+P = 128
+PACK = 4
+HALVES, XS, CLASSES = 2, 64, 4
+OCTETS, QUADS = 4, 2
+M_TILE = 128
+M_TILES = N3 // M_TILE
+
+FLOPS = 2 * N1 * N2 * N3 * R
+BYTES = 2 * (N1 * N2 * N3 + N1 * R + N2 * R) + 4 * N3 * R
+
+
+def group_by_four(copy, grouped, rows):
+    copy(
+        out=grouped.rearrange("p (c i) t -> p c t i", i=4),
+        in_=rows.rearrange("p t (c i) -> p c t i", i=4),
+    )
+
+
+def tile_recon_loss_pa_k_kernel(tc, X, A, B, C, grad_out, out):
+    nc = tc.nc
+
+    g_view = grad_out.rearrange(
+        "(half x cls) (octet quad t) n -> half cls octet quad x t n",
+        half=HALVES, x=XS, cls=CLASSES, octet=OCTETS, quad=QUADS, t=PACK,
+    )
+    a_view = A.rearrange("(half x cls) r -> half x cls r", half=HALVES, x=XS, cls=CLASSES)
+    b_view = B.rearrange("(octet quad t) r -> octet quad t r", octet=OCTETS, quad=QUADS, t=PACK)
+
+    with (
+        tc.tile_pool(name="keep", bufs=1) as keep,
+        tc.tile_pool(name="a_rows", bufs=2) as a_rows_pool,
+        tc.tile_pool(name="a_pairs", bufs=2) as a_pairs_pool,
+        tc.tile_pool(name="b_rows", bufs=2) as b_rows_pool,
+        tc.tile_pool(name="g_rows", bufs=8) as g_rows_pool,
+        tc.tile_pool(name="grouped", bufs=3) as grouped_pool,
+        tc.tile_pool(name="quantised", bufs=3) as quantised_pool,
+        tc.tile_pool(name="result", bufs=M_TILES) as result_pool,
+        tc.psum_pool(name="acc", bufs=1) as acc_pool,
+    ):
+        b_grouped = keep.tile([P, OCTETS, R, PACK], BF16)
+        acc = [acc_pool.tile([M_TILE, R], F32, name="acc%d" % m) for m in range(M_TILES)]
+
+        for half in range(HALVES):
+            a_rows = a_rows_pool.tile([P, CLASSES, R], BF16)
+            for quad in range(QUADS):
+                nc.sync.dma_start(out=a_rows[quad:P:QUADS], in_=a_view[half])
+
+            for cls in range(CLASSES):
+                a_pairs = a_pairs_pool.tile([P, R, 2], BF16)
+                nc.scalar.copy(
+                    out=a_pairs[:],
+                    in_=a_rows[:, cls, :].unsqueeze(2).to_broadcast([P, R, 2]),
+                )
+
+                for octet in range(OCTETS):
+                    first_pass = half == 0 and cls == 0 and octet == 0
+                    last_pass = half == HALVES - 1 and cls == CLASSES - 1 and octet == OCTETS - 1
+
+                    g_rows = g_rows_pool.tile([P, PACK, N3], BF16)
+                    for quad in range(QUADS):
+                        nc.sync.dma_start(
+                            out=g_rows[quad:P:QUADS], in_=g_view[half, cls, octet, quad]
+                        )
+
+                    if half == 0 and cls == 0:
+                        b_rows = b_rows_pool.tile([P, PACK, R], BF16)
+                        for quad in range(QUADS):
+                            nc.sync.dma_start(
+                                out=b_rows[quad:P:QUADS],
+                                in_=b_view[octet, quad].unsqueeze(0).to_broadcast([XS, PACK, R]),
+                            )
+                        group_by_four(nc.vector.tensor_copy, b_grouped[:, octet], b_rows[:])
+
+                    g_grouped = grouped_pool.tile([P, N3, PACK], BF16, align_bytes=64)
+                    group_by_four(nc.scalar.copy, g_grouped[:], g_rows[:])
+
+                    p_grouped = grouped_pool.tile([P, R, PACK], BF16, align_bytes=64)
+                    nc.vector.tensor_tensor(
+                        out=p_grouped[:].rearrange("p r (u e) -> p r u e", e=2),
+                        in0=a_pairs[:].unsqueeze(2).to_broadcast([P, R, 2, 2]),
+                        in1=b_grouped[:, octet].rearrange("p r (u e) -> p r u e", e=2),
+                        op=mybir.AluOpType.mult,
+                    )
+
+                    g_codes = quantised_pool.tile([P, N3], U32, align_bytes=64)
+                    g_scales = quantised_pool.tile([P, N3], U8, align_bytes=64)
+                    nc.vector.quantize_mx(
+                        out=g_codes[:].bitcast(E5M2_X4),
+                        scales=g_scales[:],
+                        in_=g_grouped[:].rearrange("p n t -> p (n t)"),
+                    )
+                    p_codes = quantised_pool.tile([P, R], U32, align_bytes=64)
+                    p_scales = quantised_pool.tile([P, R], U8, align_bytes=64)
+                    nc.vector.quantize_mx(
+                        out=p_codes[:].bitcast(E4M3_X4),
+                        scales=p_scales[:],
+                        in_=p_grouped[:].rearrange("p r t -> p (r t)"),
+                    )
+
+                    for m in range(M_TILES):
+                        m_cols = slice(m * M_TILE, (m + 1) * M_TILE)
+                        nc.tensor.matmul_mx(
+                            out=acc[m][:],
+                            lhsT=g_codes[:, m_cols].bitcast(E5M2_X4),
+                            lhsT_scale=g_scales[:, m_cols],
+                            rhs=p_codes[:].bitcast(E4M3_X4),
+                            rhs_scale=p_scales[:],
+                            start=first_pass,
+                            stop=last_pass,
+                        )
+
+        for m in range(M_TILES):
+            result = result_pool.tile([M_TILE, R], F32)
+            if m % 2 == 0:
+                nc.vector.tensor_copy(out=result[:], in_=acc[m][:])
+            else:
+                nc.scalar.copy(out=result[:], in_=acc[m][:])
+            nc.sync.dma_start(out=out[m * M_TILE : (m + 1) * M_TILE, :], in_=result[:])

@@ -42,10 +42,11 @@ def tile_recon_loss_pa_k_kernel(tc, X, A, B, C, grad_out, out):
         tc.tile_pool(name="a_pairs", bufs=2) as a_pairs_pool,
         tc.tile_pool(name="b_rows", bufs=2) as b_rows_pool,
         tc.tile_pool(name="g_rows", bufs=8) as g_rows_pool,
-        tc.tile_pool(name="grouped", bufs=3) as grouped_pool,
-        tc.tile_pool(name="quantised", bufs=3) as quantised_pool,
+        tc.tile_pool(name="grouped", bufs=6) as grouped_pool,
+        tc.tile_pool(name="quantised", bufs=4) as quantised_pool,
         tc.tile_pool(name="result", bufs=M_TILES) as result_pool,
         tc.psum_pool(name="acc", bufs=1) as acc_pool,
+        tc.manual_schedule(),
     ):
         b_grouped = keep.tile([P, OCTETS, R, PACK], BF16)
         acc = [acc_pool.tile([M_TILE, R], F32, name="acc%d" % m) for m in range(M_TILES)]

@@ -1,4 +1,5 @@
 import concourse.mybir as mybir
+from concourse.masks import make_identity
 
 BF16 = mybir.dt.bfloat16
 F32 = mybir.dt.float32
@@ -12,6 +13,8 @@ P = 128
 PACK = 4
 HALVES, XS, CLASSES = 2, 64, 4
 OCTETS, QUADS = 4, 2
+GROUPS = CLASSES * HALVES
+PASSES = GROUPS * OCTETS
 M_TILE = 128
 M_TILES = N3 // M_TILE
 
@@ -33,92 +36,119 @@ def tile_recon_loss_pa_k_kernel(tc, X, A, B, C, grad_out, out):
         "(half x cls) (octet quad t) n -> half cls octet quad x t n",
         half=HALVES, x=XS, cls=CLASSES, octet=OCTETS, quad=QUADS, t=PACK,
     )
-    a_view = A.rearrange("(half x cls) r -> half x cls r", half=HALVES, x=XS, cls=CLASSES)
+    a_view = A.rearrange("(k cls) r -> cls k r", cls=CLASSES)
     b_view = B.rearrange("(octet quad t) r -> octet quad t r", octet=OCTETS, quad=QUADS, t=PACK)
 
     with (
         tc.tile_pool(name="keep", bufs=1) as keep,
         tc.tile_pool(name="a_rows", bufs=2) as a_rows_pool,
-        tc.tile_pool(name="a_pairs", bufs=2) as a_pairs_pool,
         tc.tile_pool(name="b_rows", bufs=2) as b_rows_pool,
         tc.tile_pool(name="g_rows", bufs=8) as g_rows_pool,
         tc.tile_pool(name="grouped", bufs=6) as grouped_pool,
         tc.tile_pool(name="quantised", bufs=4) as quantised_pool,
         tc.tile_pool(name="result", bufs=M_TILES) as result_pool,
         tc.psum_pool(name="acc", bufs=1) as acc_pool,
+        tc.psum_pool(name="a_pairs", bufs=2) as a_pairs_pool,
         tc.manual_schedule(),
     ):
         b_grouped = keep.tile([P, OCTETS, R, PACK], BF16)
         acc = [acc_pool.tile([M_TILE, R], F32, name="acc%d" % m) for m in range(M_TILES)]
 
-        for half in range(HALVES):
-            a_rows = a_rows_pool.tile([P, CLASSES, R], BF16)
-            for quad in range(QUADS):
-                nc.sync.dma_start(out=a_rows[quad:P:QUADS], in_=a_view[half])
+        identity = keep.tile([P, P], BF16)
+        make_identity(nc, identity[:])
+        spread = keep.tile([P, P * QUADS], BF16)
+        nc.vector.tensor_copy(
+            out=spread[:].rearrange("k (c quad) -> k c quad", quad=QUADS),
+            in_=identity[:].unsqueeze(2).to_broadcast([P, P, QUADS]),
+        )
 
-            for cls in range(CLASSES):
-                a_pairs = a_pairs_pool.tile([P, R, 2], BF16)
-                nc.scalar.copy(
-                    out=a_pairs[:],
-                    in_=a_rows[:, cls, :].unsqueeze(2).to_broadcast([P, R, 2]),
+        def group_b(octet):
+            b_rows = b_rows_pool.tile([P, PACK, R], BF16)
+            for quad in range(QUADS):
+                nc.sync.dma_start(
+                    out=b_rows[quad:P:QUADS],
+                    in_=b_view[octet, quad].unsqueeze(0).to_broadcast([XS, PACK, R]),
+                )
+            group_by_four(nc.vector.tensor_copy, b_grouped[:, octet], b_rows[:])
+
+        a_rows_of = {}
+
+        def double_a(group):
+            cls, half = group // HALVES, group % HALVES
+            if half == 0:
+                a_rows_of[cls] = a_rows_pool.tile([P, R], BF16, name="a_rows")
+                nc.sync.dma_start(out=a_rows_of[cls][:], in_=a_view[cls])
+            a_pairs = a_pairs_pool.tile([P, R, 2], BF16)
+            for r_cols in (slice(0, R // 2), slice(R // 2, R)):
+                nc.tensor.matmul(
+                    out=a_pairs[:, r_cols, :],
+                    lhsT=spread[:, half * P : (half + 1) * P],
+                    rhs=a_rows_of[cls][:, r_cols].unsqueeze(2).to_broadcast([P, R // 2, 2]),
+                    start=True,
+                    stop=True,
+                )
+            return a_pairs
+
+        def build(half, cls, octet, a_pairs):
+            g_rows = g_rows_pool.tile([P, PACK, N3], BF16)
+            for quad in range(QUADS):
+                nc.sync.dma_start(out=g_rows[quad:P:QUADS], in_=g_view[half, cls, octet, quad])
+            g_grouped = grouped_pool.tile([P, N3, PACK], BF16, align_bytes=64)
+            group_by_four(nc.scalar.copy, g_grouped[:], g_rows[:])
+
+            p_grouped = grouped_pool.tile([P, R, PACK], BF16, align_bytes=64)
+            nc.vector.tensor_tensor(
+                out=p_grouped[:].rearrange("p r (u e) -> p r u e", e=2),
+                in0=a_pairs[:].unsqueeze(2).to_broadcast([P, R, 2, 2]),
+                in1=b_grouped[:, octet].rearrange("p r (u e) -> p r u e", e=2),
+                op=mybir.AluOpType.mult,
+            )
+            return g_grouped, p_grouped
+
+        def contract(g_grouped, p_grouped, first_pass, last_pass):
+            g_codes = quantised_pool.tile([P, N3], U32, align_bytes=64)
+            g_scales = quantised_pool.tile([P, N3], U8, align_bytes=64)
+            nc.vector.quantize_mx(
+                out=g_codes[:].bitcast(E5M2_X4),
+                scales=g_scales[:],
+                in_=g_grouped[:].rearrange("p n t -> p (n t)"),
+            )
+            p_codes = quantised_pool.tile([P, R], U32, align_bytes=64)
+            p_scales = quantised_pool.tile([P, R], U8, align_bytes=64)
+            nc.vector.quantize_mx(
+                out=p_codes[:].bitcast(E4M3_X4),
+                scales=p_scales[:],
+                in_=p_grouped[:].rearrange("p r t -> p (r t)"),
+            )
+            for m in range(M_TILES):
+                m_cols = slice(m * M_TILE, (m + 1) * M_TILE)
+                nc.tensor.matmul_mx(
+                    out=acc[m][:],
+                    lhsT=g_codes[:, m_cols].bitcast(E5M2_X4),
+                    lhsT_scale=g_scales[:, m_cols],
+                    rhs=p_codes[:].bitcast(E4M3_X4),
+                    rhs_scale=p_scales[:],
+                    start=first_pass,
+                    stop=last_pass,
                 )
 
-                for octet in range(OCTETS):
-                    first_pass = half == 0 and cls == 0 and octet == 0
-                    last_pass = half == HALVES - 1 and cls == CLASSES - 1 and octet == OCTETS - 1
-
-                    g_rows = g_rows_pool.tile([P, PACK, N3], BF16)
-                    for quad in range(QUADS):
-                        nc.sync.dma_start(
-                            out=g_rows[quad:P:QUADS], in_=g_view[half, cls, octet, quad]
-                        )
-
-                    if half == 0 and cls == 0:
-                        b_rows = b_rows_pool.tile([P, PACK, R], BF16)
-                        for quad in range(QUADS):
-                            nc.sync.dma_start(
-                                out=b_rows[quad:P:QUADS],
-                                in_=b_view[octet, quad].unsqueeze(0).to_broadcast([XS, PACK, R]),
-                            )
-                        group_by_four(nc.vector.tensor_copy, b_grouped[:, octet], b_rows[:])
-
-                    g_grouped = grouped_pool.tile([P, N3, PACK], BF16, align_bytes=64)
-                    group_by_four(nc.scalar.copy, g_grouped[:], g_rows[:])
-
-                    p_grouped = grouped_pool.tile([P, R, PACK], BF16, align_bytes=64)
-                    nc.vector.tensor_tensor(
-                        out=p_grouped[:].rearrange("p r (u e) -> p r u e", e=2),
-                        in0=a_pairs[:].unsqueeze(2).to_broadcast([P, R, 2, 2]),
-                        in1=b_grouped[:, octet].rearrange("p r (u e) -> p r u e", e=2),
-                        op=mybir.AluOpType.mult,
-                    )
-
-                    g_codes = quantised_pool.tile([P, N3], U32, align_bytes=64)
-                    g_scales = quantised_pool.tile([P, N3], U8, align_bytes=64)
-                    nc.vector.quantize_mx(
-                        out=g_codes[:].bitcast(E5M2_X4),
-                        scales=g_scales[:],
-                        in_=g_grouped[:].rearrange("p n t -> p (n t)"),
-                    )
-                    p_codes = quantised_pool.tile([P, R], U32, align_bytes=64)
-                    p_scales = quantised_pool.tile([P, R], U8, align_bytes=64)
-                    nc.vector.quantize_mx(
-                        out=p_codes[:].bitcast(E4M3_X4),
-                        scales=p_scales[:],
-                        in_=p_grouped[:].rearrange("p r t -> p (r t)"),
-                    )
-
-                    for m in range(M_TILES):
-                        m_cols = slice(m * M_TILE, (m + 1) * M_TILE)
-                        nc.tensor.matmul_mx(
-                            out=acc[m][:],
-                            lhsT=g_codes[:, m_cols].bitcast(E5M2_X4),
-                            lhsT_scale=g_scales[:, m_cols],
-                            rhs=p_codes[:].bitcast(E4M3_X4),
-                            rhs_scale=p_scales[:],
-                            start=first_pass,
-                            stop=last_pass,
-                        )
+        a_pairs = None
+        a_pairs_ahead = double_a(0)
+        built = None
+        for s in range(PASSES + 1):
+            previous = built
+            if s < PASSES:
+                group, octet = s // OCTETS, s % OCTETS
+                cls, half = group // HALVES, group % HALVES
+                if group == 0:
+                    group_b(octet)
+                if octet == 0:
+                    a_pairs = a_pairs_ahead
+                    if group + 1 < GROUPS:
+                        a_pairs_ahead = double_a(group + 1)
+                built = build(half, cls, octet, a_pairs)
+            if previous is not None:
+                contract(previous[0], previous[1], first_pass=s == 1, last_pass=s == PASSES)
 
         for m in range(M_TILES):
             result = result_pool.tile([M_TILE, R], F32)

@@ -17,6 +17,8 @@ GROUPS = CLASSES * HALVES
 PASSES = GROUPS * OCTETS
 M_TILE = 128
 M_TILES = N3 // M_TILE
+GP_R = 64
+V_R = R - GP_R
 
 FLOPS = 2 * N1 * N2 * N3 * R
 BYTES = 2 * (N1 * N2 * N3 + N1 * R + N2 * R) + 4 * N3 * R
@@ -45,6 +47,7 @@ def tile_recon_loss_pa_k_kernel(tc, X, A, B, C, grad_out, out):
         tc.tile_pool(name="b_rows", bufs=2) as b_rows_pool,
         tc.tile_pool(name="g_rows", bufs=8) as g_rows_pool,
         tc.tile_pool(name="grouped", bufs=6) as grouped_pool,
+        tc.tile_pool(name="product", bufs=2) as product_pool,
         tc.tile_pool(name="quantised", bufs=4) as quantised_pool,
         tc.tile_pool(name="result", bufs=M_TILES) as result_pool,
         tc.psum_pool(name="acc", bufs=1) as acc_pool,
@@ -61,6 +64,14 @@ def tile_recon_loss_pa_k_kernel(tc, X, A, B, C, grad_out, out):
             out=spread[:].rearrange("k (c quad) -> k c quad", quad=QUADS),
             in_=identity[:].unsqueeze(2).to_broadcast([P, P, QUADS]),
         )
+
+        a_small = keep.tile([P, HALVES, CLASSES, GP_R], BF16)
+        a_small_view = A.rearrange("(half x cls) r -> half x cls r", half=HALVES, x=XS, cls=CLASSES)
+        for half in range(HALVES):
+            for quad in range(QUADS):
+                nc.scalar.dma_start(
+                    out=a_small[quad:P:QUADS, half], in_=a_small_view[half][:, :, V_R:R]
+                )
 
         def group_b(octet):
             b_rows = b_rows_pool.tile([P, PACK, R], BF16)
@@ -96,11 +107,17 @@ def tile_recon_loss_pa_k_kernel(tc, X, A, B, C, grad_out, out):
             g_grouped = grouped_pool.tile([P, N3, PACK], BF16, align_bytes=64)
             group_by_four(nc.scalar.copy, g_grouped[:], g_rows[:])
 
-            p_grouped = grouped_pool.tile([P, R, PACK], BF16, align_bytes=64)
+            p_grouped = product_pool.tile([P, R, PACK], BF16, align_bytes=64)
             nc.vector.tensor_tensor(
-                out=p_grouped[:].rearrange("p r (u e) -> p r u e", e=2),
-                in0=a_pairs[:].unsqueeze(2).to_broadcast([P, R, 2, 2]),
-                in1=b_grouped[:, octet].rearrange("p r (u e) -> p r u e", e=2),
+                out=p_grouped[:, :V_R].rearrange("p r (u e) -> p r u e", e=2),
+                in0=a_pairs[:, :V_R].unsqueeze(2).to_broadcast([P, V_R, 2, 2]),
+                in1=b_grouped[:, octet, :V_R].rearrange("p r (u e) -> p r u e", e=2),
+                op=mybir.AluOpType.mult,
+            )
+            nc.gpsimd.tensor_tensor(
+                out=p_grouped[:, V_R:],
+                in0=a_small[:, half, cls].unsqueeze(2).to_broadcast([P, GP_R, PACK]),
+                in1=b_grouped[:, octet, V_R:],
                 op=mybir.AluOpType.mult,
             )
             return g_grouped, p_grouped

@@ -123,19 +123,19 @@ def tile_recon_loss_pa_k_kernel(tc, X, A, B, C, grad_out, out):
             return g_grouped, p_grouped
 
         def contract(g_grouped, p_grouped, first_pass, last_pass):
-            g_codes = quantised_pool.tile([P, N3], U32, align_bytes=64)
-            g_scales = quantised_pool.tile([P, N3], U8, align_bytes=64)
-            nc.vector.quantize_mx(
-                out=g_codes[:].bitcast(E5M2_X4),
-                scales=g_scales[:],
-                in_=g_grouped[:].rearrange("p n t -> p (n t)"),
-            )
             p_codes = quantised_pool.tile([P, R], U32, align_bytes=64)
             p_scales = quantised_pool.tile([P, R], U8, align_bytes=64)
             nc.vector.quantize_mx(
                 out=p_codes[:].bitcast(E4M3_X4),
                 scales=p_scales[:],
                 in_=p_grouped[:].rearrange("p r t -> p (r t)"),
+            )
+            g_codes = quantised_pool.tile([P, N3], U32, align_bytes=64)
+            g_scales = quantised_pool.tile([P, N3], U8, align_bytes=64)
+            nc.vector.quantize_mx(
+                out=g_codes[:].bitcast(E5M2_X4),
+                scales=g_scales[:],
+                in_=g_grouped[:].rearrange("p n t -> p (n t)"),
             )
             for m in range(M_TILES):
                 m_cols = slice(m * M_TILE, (m + 1) * M_TILE)

@@ -15,9 +15,13 @@ HALVES, XS, CLASSES = 2, 64, 4
 OCTETS, QUADS = 4, 2
 GROUPS = CLASSES * HALVES
 PASSES = GROUPS * OCTETS
+PAIR = 2
+ROUNDS = PASSES // PAIR
+ROUNDS_A_GROUP = OCTETS // PAIR
+ROUNDS_AHEAD = 2
 M_TILE = 128
 M_TILES = N3 // M_TILE
-GP_R = 64
+GP_R = 88
 V_R = R - GP_R
 
 FLOPS = 2 * N1 * N2 * N3 * R
@@ -46,9 +50,10 @@ def tile_recon_loss_pa_k_kernel(tc, X, A, B, C, grad_out, out):
         tc.tile_pool(name="a_rows", bufs=2) as a_rows_pool,
         tc.tile_pool(name="b_rows", bufs=2) as b_rows_pool,
         tc.tile_pool(name="g_rows", bufs=8) as g_rows_pool,
-        tc.tile_pool(name="grouped", bufs=6) as grouped_pool,
+        tc.tile_pool(name="grouped", bufs=8) as grouped_pool,
         tc.tile_pool(name="product", bufs=2) as product_pool,
         tc.tile_pool(name="quantised", bufs=4) as quantised_pool,
+        tc.tile_pool(name="p_quantised", bufs=3) as p_quantised_pool,
         tc.tile_pool(name="result", bufs=M_TILES) as result_pool,
         tc.psum_pool(name="acc", bufs=1) as acc_pool,
         tc.psum_pool(name="a_pairs", bufs=2) as a_pairs_pool,
@@ -100,36 +105,38 @@ def tile_recon_loss_pa_k_kernel(tc, X, A, B, C, grad_out, out):
                 )
             return a_pairs
 
-        def build(half, cls, octet, a_pairs):
+        def regroup_g(s):
+            group, octet = s // OCTETS, s % OCTETS
+            cls, half = group // HALVES, group % HALVES
             g_rows = g_rows_pool.tile([P, PACK, N3], BF16)
             for quad in range(QUADS):
                 nc.sync.dma_start(out=g_rows[quad:P:QUADS], in_=g_view[half, cls, octet, quad])
             g_grouped = grouped_pool.tile([P, N3, PACK], BF16, align_bytes=64)
             group_by_four(nc.scalar.copy, g_grouped[:], g_rows[:])
+            return g_grouped
 
-            p_grouped = product_pool.tile([P, R, PACK], BF16, align_bytes=64)
+        def multiply_on_vector(p_grouped, which, octet, a_pairs):
             nc.vector.tensor_tensor(
-                out=p_grouped[:, :V_R].rearrange("p r (u e) -> p r u e", e=2),
+                out=p_grouped[:, which, :V_R].rearrange("p r (u e) -> p r u e", e=2),
                 in0=a_pairs[:, :V_R].unsqueeze(2).to_broadcast([P, V_R, 2, 2]),
                 in1=b_grouped[:, octet, :V_R].rearrange("p r (u e) -> p r u e", e=2),
                 op=mybir.AluOpType.mult,
             )
+
+        def multiply_on_gpsimd(p_grouped, which, octets, group):
+            cls, half = group // HALVES, group % HALVES
+            count = octets.stop - octets.start
             nc.gpsimd.tensor_tensor(
-                out=p_grouped[:, V_R:],
-                in0=a_small[:, half, cls].unsqueeze(2).to_broadcast([P, GP_R, PACK]),
-                in1=b_grouped[:, octet, V_R:],
+                out=p_grouped[:, which, V_R:],
+                in0=a_small[:, half, cls]
+                .unsqueeze(1)
+                .unsqueeze(3)
+                .to_broadcast([P, count, GP_R, PACK]),
+                in1=b_grouped[:, octets, V_R:],
                 op=mybir.AluOpType.mult,
             )
-            return g_grouped, p_grouped
 
-        def contract(g_grouped, p_grouped, first_pass, last_pass):
-            p_codes = quantised_pool.tile([P, R], U32, align_bytes=64)
-            p_scales = quantised_pool.tile([P, R], U8, align_bytes=64)
-            nc.vector.quantize_mx(
-                out=p_codes[:].bitcast(E4M3_X4),
-                scales=p_scales[:],
-                in_=p_grouped[:].rearrange("p r t -> p (r t)"),
-            )
+        def quantise_g(g_grouped):
             g_codes = quantised_pool.tile([P, N3], U32, align_bytes=64)
             g_scales = quantised_pool.tile([P, N3], U8, align_bytes=64)
             nc.vector.quantize_mx(
@@ -137,35 +144,70 @@ def tile_recon_loss_pa_k_kernel(tc, X, A, B, C, grad_out, out):
                 scales=g_scales[:],
                 in_=g_grouped[:].rearrange("p n t -> p (n t)"),
             )
+            return g_codes, g_scales
+
+        def quantise_p(p_grouped):
+            p_codes = p_quantised_pool.tile([P, PAIR, R], U32, align_bytes=64)
+            p_scales = p_quantised_pool.tile([P, PAIR, R], U8, align_bytes=64)
+            nc.vector.quantize_mx(
+                out=p_codes[:].rearrange("p o r -> p (o r)").bitcast(E4M3_X4),
+                scales=p_scales[:].rearrange("p o r -> p (o r)"),
+                in_=p_grouped[:].rearrange("p o r t -> p (o r t)"),
+            )
+            return p_codes, p_scales
+
+        def contract(g_quantised, p_quantised, which, first_pass, last_pass):
+            g_codes, g_scales = g_quantised
+            p_codes, p_scales = p_quantised
             for m in range(M_TILES):
                 m_cols = slice(m * M_TILE, (m + 1) * M_TILE)
                 nc.tensor.matmul_mx(
                     out=acc[m][:],
                     lhsT=g_codes[:, m_cols].bitcast(E5M2_X4),
                     lhsT_scale=g_scales[:, m_cols],
-                    rhs=p_codes[:].bitcast(E4M3_X4),
-                    rhs_scale=p_scales[:],
+                    rhs=p_codes[:, which].bitcast(E4M3_X4),
+                    rhs_scale=p_scales[:, which],
                     start=first_pass,
                     stop=last_pass,
                 )
 
-        a_pairs = None
-        a_pairs_ahead = double_a(0)
-        built = None
-        for s in range(PASSES + 1):
-            previous = built
-            if s < PASSES:
-                group, octet = s // OCTETS, s % OCTETS
-                cls, half = group // HALVES, group % HALVES
-                if group == 0:
-                    group_b(octet)
-                if octet == 0:
-                    a_pairs = a_pairs_ahead
-                    if group + 1 < GROUPS:
-                        a_pairs_ahead = double_a(group + 1)
-                built = build(half, cls, octet, a_pairs)
-            if previous is not None:
-                contract(previous[0], previous[1], first_pass=s == 1, last_pass=s == PASSES)
+        a_pairs_of = {0: double_a(0), 1: double_a(1)}
+        g_grouped_of = {}
+        product_of = {}
+
+        for rnd in range(ROUNDS_AHEAD):
+            product_of[rnd] = product_pool.tile([P, PAIR, R, PACK], BF16, align_bytes=64, name="p_grouped")
+            for which in range(PAIR):
+                octet = PAIR * rnd + which
+                group_b(octet)
+                g_grouped_of[octet] = regroup_g(octet)
+                multiply_on_vector(product_of[rnd], which, octet, a_pairs_of[0])
+                multiply_on_gpsimd(
+                    product_of[rnd], slice(which, which + 1), slice(octet, octet + 1), 0
+                )
+
+        for rnd in range(ROUNDS):
+            first, second = PAIR * rnd, PAIR * rnd + 1
+            if rnd % ROUNDS_A_GROUP == 0 and rnd // ROUNDS_A_GROUP + 2 < GROUPS:
+                a_pairs_of[rnd // ROUNDS_A_GROUP + 2] = double_a(rnd // ROUNDS_A_GROUP + 2)
+            for s in (first + PAIR * ROUNDS_AHEAD, second + PAIR * ROUNDS_AHEAD):
+                if s < PASSES:
+                    g_grouped_of[s] = regroup_g(s)
+            g_first = quantise_g(g_grouped_of[first])
+            p_both = quantise_p(product_of[rnd])
+            contract(g_first, p_both, 0, first_pass=first == 0, last_pass=False)
+            g_second = quantise_g(g_grouped_of[second])
+            contract(g_second, p_both, 1, first_pass=False, last_pass=second == PASSES - 1)
+            ahead = rnd + ROUNDS_AHEAD
+            if ahead < ROUNDS:
+                group = ahead // ROUNDS_A_GROUP
+                octet = PAIR * (ahead % ROUNDS_A_GROUP)
+                product_of[ahead] = product_pool.tile([P, PAIR, R, PACK], BF16, align_bytes=64, name="p_grouped")
+                for which in range(PAIR):
+                    multiply_on_vector(product_of[ahead], which, octet + which, a_pairs_of[group])
+                multiply_on_gpsimd(
+                    product_of[ahead], slice(0, PAIR), slice(octet, octet + PAIR), group
+                )
 
         for m in range(M_TILES):
             result = result_pool.tile([M_TILE, R], F32)

@@ -21,6 +21,7 @@ ROUNDS_A_GROUP = OCTETS // PAIR
 ROUNDS_AHEAD = 2
 M_TILE = 128
 M_TILES = N3 // M_TILE
+PE_OCTET = 1
 GP_R = 88
 V_R = R - GP_R
 
@@ -57,6 +58,7 @@ def tile_recon_loss_pa_k_kernel(tc, X, A, B, C, grad_out, out):
         tc.tile_pool(name="result", bufs=M_TILES) as result_pool,
         tc.psum_pool(name="acc", bufs=1) as acc_pool,
         tc.psum_pool(name="a_pairs", bufs=2) as a_pairs_pool,
+        tc.psum_pool(name="g_bank", bufs=2) as g_bank_pool,
         tc.manual_schedule(),
     ):
         b_grouped = keep.tile([P, OCTETS, R, PACK], BF16)
@@ -112,7 +114,21 @@ def tile_recon_loss_pa_k_kernel(tc, X, A, B, C, grad_out, out):
             for quad in range(QUADS):
                 nc.sync.dma_start(out=g_rows[quad:P:QUADS], in_=g_view[half, cls, octet, quad])
             g_grouped = grouped_pool.tile([P, N3, PACK], BF16, align_bytes=64)
-            group_by_four(nc.scalar.copy, g_grouped[:], g_rows[:])
+            if octet == PE_OCTET and group > 0:
+                for bank_cols in (slice(0, N3 // 2), slice(N3 // 2, N3)):
+                    g_bank = g_bank_pool.tile([P, N3 // 2, PACK], BF16)
+                    for part in range(2):
+                        n0 = bank_cols.start + part * M_TILE
+                        nc.tensor.matmul(
+                            out=g_bank[:, part * M_TILE : (part + 1) * M_TILE, :],
+                            lhsT=identity[:],
+                            rhs=g_rows[:, :, n0 : n0 + M_TILE].rearrange("p t n -> p n t"),
+                            start=True,
+                            stop=True,
+                        )
+                    nc.scalar.copy(out=g_grouped[:, bank_cols, :], in_=g_bank[:])
+            else:
+                group_by_four(nc.scalar.copy, g_grouped[:], g_rows[:])
             return g_grouped
 
         def multiply_on_vector(p_grouped, which, octet, a_pairs):
@@ -190,14 +206,14 @@ def tile_recon_loss_pa_k_kernel(tc, X, A, B, C, grad_out, out):
             first, second = PAIR * rnd, PAIR * rnd + 1
             if rnd % ROUNDS_A_GROUP == 0 and rnd // ROUNDS_A_GROUP + 2 < GROUPS:
                 a_pairs_of[rnd // ROUNDS_A_GROUP + 2] = double_a(rnd // ROUNDS_A_GROUP + 2)
-            for s in (first + PAIR * ROUNDS_AHEAD, second + PAIR * ROUNDS_AHEAD):
-                if s < PASSES:
-                    g_grouped_of[s] = regroup_g(s)
             g_first = quantise_g(g_grouped_of[first])
             p_both = quantise_p(product_of[rnd])
             contract(g_first, p_both, 0, first_pass=first == 0, last_pass=False)
             g_second = quantise_g(g_grouped_of[second])
             contract(g_second, p_both, 1, first_pass=False, last_pass=second == PASSES - 1)
+            for s in (first + PAIR * ROUNDS_AHEAD, second + PAIR * ROUNDS_AHEAD):
+                if s < PASSES:
+                    g_grouped_of[s] = regroup_g(s)
             ahead = rnd + ROUNDS_AHEAD
             if ahead < ROUNDS:
                 group = ahead // ROUNDS_A_GROUP

@@ -29,10 +29,10 @@ FLOPS = 2 * N1 * N2 * N3 * R
 BYTES = 2 * (N1 * N2 * N3 + N1 * R + N2 * R) + 4 * N3 * R
 
 
-def group_by_four(copy, grouped, rows):
+def group_by_four(copy, grouped, rows, run=4):
     copy(
-        out=grouped.rearrange("p (c i) t -> p c t i", i=4),
-        in_=rows.rearrange("p t (c i) -> p c t i", i=4),
+        out=grouped.rearrange("p (c i) t -> p c t i", i=run),
+        in_=rows.rearrange("p t (c i) -> p c t i", i=run),
     )
 
 
@@ -128,7 +128,7 @@ def tile_recon_loss_pa_k_kernel(tc, X, A, B, C, grad_out, out):
                         )
                     nc.scalar.copy(out=g_grouped[:, bank_cols, :], in_=g_bank[:])
             else:
-                group_by_four(nc.scalar.copy, g_grouped[:], g_rows[:])
+                group_by_four(nc.scalar.copy, g_grouped[:], g_rows[:], run=8)
             return g_grouped
 
         def multiply_on_vector(p_grouped, which, octet, a_pairs):

import concourse.mybir as mybir
from concourse.masks import make_identity

BF16 = mybir.dt.bfloat16
F32 = mybir.dt.float32
U32 = mybir.dt.uint32
U8 = mybir.dt.uint8
E4M3_X4 = mybir.dt.float8_e4m3fn_x4
E5M2_X4 = mybir.dt.float8_e5m2_x4

N1, N2, N3, R = 512, 32, 512, 512
P = 128
PACK = 4
HALVES, XS, CLASSES = 2, 64, 4
OCTETS, QUADS = 4, 2
GROUPS = CLASSES * HALVES
PASSES = GROUPS * OCTETS
PAIR = 2
ROUNDS = PASSES // PAIR
ROUNDS_A_GROUP = OCTETS // PAIR
ROUNDS_AHEAD = 2
M_TILE = 128
M_TILES = N3 // M_TILE
PE_OCTET = 1
GP_R = 88
V_R = R - GP_R

FLOPS = 2 * N1 * N2 * N3 * R
BYTES = 2 * (N1 * N2 * N3 + N1 * R + N2 * R) + 4 * N3 * R


def group_by_four(copy, grouped, rows, run=4):
    copy(
        out=grouped.rearrange("p (c i) t -> p c t i", i=run),
        in_=rows.rearrange("p t (c i) -> p c t i", i=run),
    )


def tile_recon_loss_pa_k_kernel(tc, X, A, B, C, grad_out, out):
    nc = tc.nc

    g_view = grad_out.rearrange(
        "(half x cls) (octet quad t) n -> half cls octet quad x t n",
        half=HALVES, x=XS, cls=CLASSES, octet=OCTETS, quad=QUADS, t=PACK,
    )
    a_view = A.rearrange("(k cls) r -> cls k r", cls=CLASSES)
    b_view = B.rearrange("(octet quad t) r -> octet quad t r", octet=OCTETS, quad=QUADS, t=PACK)

    with (
        tc.tile_pool(name="keep", bufs=1) as keep,
        tc.tile_pool(name="a_rows", bufs=2) as a_rows_pool,
        tc.tile_pool(name="b_rows", bufs=2) as b_rows_pool,
        tc.tile_pool(name="g_rows", bufs=8) as g_rows_pool,
        tc.tile_pool(name="grouped", bufs=8) as grouped_pool,
        tc.tile_pool(name="product", bufs=2) as product_pool,
        tc.tile_pool(name="quantised", bufs=4) as quantised_pool,
        tc.tile_pool(name="p_quantised", bufs=3) as p_quantised_pool,
        tc.tile_pool(name="result", bufs=M_TILES) as result_pool,
        tc.psum_pool(name="acc", bufs=1) as acc_pool,
        tc.psum_pool(name="a_pairs", bufs=2) as a_pairs_pool,
        tc.psum_pool(name="g_bank", bufs=2) as g_bank_pool,
        tc.manual_schedule(),
    ):
        b_grouped = keep.tile([P, OCTETS, R, PACK], BF16)
        acc = [acc_pool.tile([M_TILE, R], F32, name="acc%d" % m) for m in range(M_TILES)]

        identity = keep.tile([P, P], BF16)
        make_identity(nc, identity[:])
        spread = keep.tile([P, P * QUADS], BF16)
        nc.vector.tensor_copy(
            out=spread[:].rearrange("k (c quad) -> k c quad", quad=QUADS),
            in_=identity[:].unsqueeze(2).to_broadcast([P, P, QUADS]),
        )

        a_small = keep.tile([P, HALVES, CLASSES, GP_R], BF16)
        a_small_view = A.rearrange("(half x cls) r -> half x cls r", half=HALVES, x=XS, cls=CLASSES)
        for half in range(HALVES):
            for quad in range(QUADS):
                nc.scalar.dma_start(
                    out=a_small[quad:P:QUADS, half], in_=a_small_view[half][:, :, V_R:R]
                )

        def group_b(octet):
            b_rows = b_rows_pool.tile([P, PACK, R], BF16)
            for quad in range(QUADS):
                nc.sync.dma_start(
                    out=b_rows[quad:P:QUADS],
                    in_=b_view[octet, quad].unsqueeze(0).to_broadcast([XS, PACK, R]),
                )
            group_by_four(nc.vector.tensor_copy, b_grouped[:, octet], b_rows[:])

        a_rows_of = {}

        def double_a(group):
            cls, half = group // HALVES, group % HALVES
            if half == 0:
                a_rows_of[cls] = a_rows_pool.tile([P, R], BF16, name="a_rows")
                nc.sync.dma_start(out=a_rows_of[cls][:], in_=a_view[cls])
            a_pairs = a_pairs_pool.tile([P, R, 2], BF16)
            for r_cols in (slice(0, R // 2), slice(R // 2, R)):
                nc.tensor.matmul(
                    out=a_pairs[:, r_cols, :],
                    lhsT=spread[:, half * P : (half + 1) * P],
                    rhs=a_rows_of[cls][:, r_cols].unsqueeze(2).to_broadcast([P, R // 2, 2]),
                    start=True,
                    stop=True,
                )
            return a_pairs

        def regroup_g(s):
            group, octet = s // OCTETS, s % OCTETS
            cls, half = group // HALVES, group % HALVES
            g_rows = g_rows_pool.tile([P, PACK, N3], BF16)
            for quad in range(QUADS):
                nc.sync.dma_start(out=g_rows[quad:P:QUADS], in_=g_view[half, cls, octet, quad])
            g_grouped = grouped_pool.tile([P, N3, PACK], BF16, align_bytes=64)
            if octet == PE_OCTET and group > 0:
                for bank_cols in (slice(0, N3 // 2), slice(N3 // 2, N3)):
                    g_bank = g_bank_pool.tile([P, N3 // 2, PACK], BF16)
                    for part in range(2):
                        n0 = bank_cols.start + part * M_TILE
                        nc.tensor.matmul(
                            out=g_bank[:, part * M_TILE : (part + 1) * M_TILE, :],
                            lhsT=identity[:],
                            rhs=g_rows[:, :, n0 : n0 + M_TILE].rearrange("p t n -> p n t"),
                            start=True,
                            stop=True,
                        )
                    nc.scalar.copy(out=g_grouped[:, bank_cols, :], in_=g_bank[:])
            else:
                group_by_four(nc.scalar.copy, g_grouped[:], g_rows[:], run=8)
            return g_grouped

        def multiply_on_vector(p_grouped, which, octet, a_pairs):
            nc.vector.tensor_tensor(
                out=p_grouped[:, which, :V_R].rearrange("p r (u e) -> p r u e", e=2),
                in0=a_pairs[:, :V_R].unsqueeze(2).to_broadcast([P, V_R, 2, 2]),
                in1=b_grouped[:, octet, :V_R].rearrange("p r (u e) -> p r u e", e=2),
                op=mybir.AluOpType.mult,
            )

        def multiply_on_gpsimd(p_grouped, which, octets, group):
            cls, half = group // HALVES, group % HALVES
            count = octets.stop - octets.start
            nc.gpsimd.tensor_tensor(
                out=p_grouped[:, which, V_R:],
                in0=a_small[:, half, cls]
                .unsqueeze(1)
                .unsqueeze(3)
                .to_broadcast([P, count, GP_R, PACK]),
                in1=b_grouped[:, octets, V_R:],
                op=mybir.AluOpType.mult,
            )

        def quantise_g(g_grouped):
            g_codes = quantised_pool.tile([P, N3], U32, align_bytes=64)
            g_scales = quantised_pool.tile([P, N3], U8, align_bytes=64)
            nc.vector.quantize_mx(
                out=g_codes[:].bitcast(E5M2_X4),
                scales=g_scales[:],
                in_=g_grouped[:].rearrange("p n t -> p (n t)"),
            )
            return g_codes, g_scales

        def quantise_p(p_grouped):
            p_codes = p_quantised_pool.tile([P, PAIR, R], U32, align_bytes=64)
            p_scales = p_quantised_pool.tile([P, PAIR, R], U8, align_bytes=64)
            nc.vector.quantize_mx(
                out=p_codes[:].rearrange("p o r -> p (o r)").bitcast(E4M3_X4),
                scales=p_scales[:].rearrange("p o r -> p (o r)"),
                in_=p_grouped[:].rearrange("p o r t -> p (o r t)"),
            )
            return p_codes, p_scales

        def contract(g_quantised, p_quantised, which, first_pass, last_pass):
            g_codes, g_scales = g_quantised
            p_codes, p_scales = p_quantised
            for m in range(M_TILES):
                m_cols = slice(m * M_TILE, (m + 1) * M_TILE)
                nc.tensor.matmul_mx(
                    out=acc[m][:],
                    lhsT=g_codes[:, m_cols].bitcast(E5M2_X4),
                    lhsT_scale=g_scales[:, m_cols],
                    rhs=p_codes[:, which].bitcast(E4M3_X4),
                    rhs_scale=p_scales[:, which],
                    start=first_pass,
                    stop=last_pass,
                )

        a_pairs_of = {0: double_a(0), 1: double_a(1)}
        g_grouped_of = {}
        product_of = {}

        for rnd in range(ROUNDS_AHEAD):
            product_of[rnd] = product_pool.tile([P, PAIR, R, PACK], BF16, align_bytes=64, name="p_grouped")
            for which in range(PAIR):
                octet = PAIR * rnd + which
                group_b(octet)
                g_grouped_of[octet] = regroup_g(octet)
                multiply_on_vector(product_of[rnd], which, octet, a_pairs_of[0])
                multiply_on_gpsimd(
                    product_of[rnd], slice(which, which + 1), slice(octet, octet + 1), 0
                )

        for rnd in range(ROUNDS):
            first, second = PAIR * rnd, PAIR * rnd + 1
            if rnd % ROUNDS_A_GROUP == 0 and rnd // ROUNDS_A_GROUP + 2 < GROUPS:
                a_pairs_of[rnd // ROUNDS_A_GROUP + 2] = double_a(rnd // ROUNDS_A_GROUP + 2)
            g_first = quantise_g(g_grouped_of[first])
            p_both = quantise_p(product_of[rnd])
            contract(g_first, p_both, 0, first_pass=first == 0, last_pass=False)
            g_second = quantise_g(g_grouped_of[second])
            contract(g_second, p_both, 1, first_pass=False, last_pass=second == PASSES - 1)
            for s in (first + PAIR * ROUNDS_AHEAD, second + PAIR * ROUNDS_AHEAD):
                if s < PASSES:
                    g_grouped_of[s] = regroup_g(s)
            ahead = rnd + ROUNDS_AHEAD
            if ahead < ROUNDS:
                group = ahead // ROUNDS_A_GROUP
                octet = PAIR * (ahead % ROUNDS_A_GROUP)
                product_of[ahead] = product_pool.tile([P, PAIR, R, PACK], BF16, align_bytes=64, name="p_grouped")
                for which in range(PAIR):
                    multiply_on_vector(product_of[ahead], which, octet + which, a_pairs_of[group])
                multiply_on_gpsimd(
                    product_of[ahead], slice(0, PAIR), slice(octet, octet + PAIR), group
                )

        for m in range(M_TILES):
            result = result_pool.tile([M_TILE, R], F32)
            if m % 2 == 0:
                nc.vector.tensor_copy(out=result[:], in_=acc[m][:])
            else:
                nc.scalar.copy(out=result[:], in_=acc[m][:])
            nc.sync.dma_start(out=out[m * M_TILE : (m + 1) * M_TILE, :], in_=result[:])
